import numpy as np
import ml_dtypes


def mxq(x, axis, fmt="e4m3"):
    dtype, down = {"e4m3": (ml_dtypes.float8_e4m3fn, 7), "e5m2": (ml_dtypes.float8_e5m2, 14)}[fmt]
    v = np.moveaxis(np.asarray(x, np.float32).astype(ml_dtypes.bfloat16).astype(np.float64), axis, -1)
    blocks = v.reshape(v.shape[:-1] + (-1, 32))
    amax = np.abs(blocks).max(-1, keepdims=True)
    byte = np.maximum(np.where(amax > 0, np.frexp(amax)[1] - 1 + 127, 0) - down, 1)
    scale = np.exp2(byte - 127.0)
    codes = (blocks / scale).astype(np.float32).astype(dtype).astype(np.float64)
    return np.moveaxis((codes * scale).reshape(v.shape), -1, axis)


WIDE = False


def mx_kscale(k):
    if not WIDE:
        return np.ones(k)
    levels = np.array([10, -10, 5, -5, 0])
    a = np.random.permutation(np.resize(levels, k // 512 * 4)).reshape(k // 512, 4)
    idx = np.arange(k)
    return np.exp2(a[idx // 512, idx % 128 // 32])


BF16 = ml_dtypes.bfloat16


def bf(x):
    return np.asarray(x, np.float32).astype(BF16)


def f64(x):
    return np.asarray(x).astype(np.float64)


B, IN, H = 512, 1024, 1024


def sigmoid(v):
    return 1.0 / (1.0 + np.exp(-v))


def setup_inputs():
    s, t = mx_kscale(IN), mx_kscale(H)
    a = np.sqrt(2.0 / (IN + H))
    d = 0.3 + np.random.standard_normal((B, H)) * 1.6
    return {
        "x": bf(np.random.standard_normal((B, IN)) * s),
        "h_prev": bf(np.random.standard_normal((B, H)) * t),
        "c_prev": bf(np.random.standard_normal((B, H))),
        "n_prev": bf(1.0 + np.random.standard_normal((B, H)) * 0.1),
        "i_prime": bf(np.exp(np.minimum(d, 0.0))),
        "f_prime": bf(np.exp(np.minimum(-d, 0.0))),
        "Wz_x": bf(np.random.standard_normal((H, IN)) * a / s),
        "b_z": bf(np.random.standard_normal(H) * 0.3),
        "Wz_h": bf(np.random.standard_normal((H, H)) * a / t),
        "Wo_x": bf(np.random.standard_normal((H, IN)) * a / s),
        "b_o": bf(np.random.standard_normal(H) * 0.3),
        "Wo_h": bf(np.random.standard_normal((H, H)) * a / t),
    }


def reference(x, h_prev, c_prev, n_prev, i_prime, f_prime, Wz_x, b_z, Wz_h, Wo_x, b_o, Wo_h):
    xq = mxq(f64(x), 1, "e4m3")
    hq = mxq(f64(h_prev), 1, "e4m3")
    z_aff = (xq @ mxq(f64(Wz_x), 1, "e4m3").T) + f64(b_z) + (hq @ mxq(f64(Wz_h), 1, "e4m3").T)
    o_aff = (xq @ mxq(f64(Wo_x), 1, "e4m3").T) + f64(b_o) + (hq @ mxq(f64(Wo_h), 1, "e4m3").T)
    z = np.tanh(z_aff)
    c_t = f64(f_prime) * f64(c_prev) + f64(i_prime) * z
    n_t = f64(f_prime) * f64(n_prev) + f64(i_prime)
    h_t = sigmoid(o_aff) * (c_t / np.maximum(n_t, 1e-6))
    return h_t, c_t

@@ -1,0 +1,239 @@
+from contextlib import ExitStack
+
+import concourse.mybir as mybir
+from concourse.masks import make_identity
+
+F32 = mybir.dt.float32
+BF16 = mybir.dt.bfloat16
+U32 = mybir.dt.uint32
+U8 = mybir.dt.uint8
+FP8X4 = mybir.dt.float8_e4m3fn_x4
+ACT = mybir.ActivationFunctionType
+ALU = mybir.AluOpType
+
+P = 128
+PACK = 4
+BATCH = 512
+FEATURES = 1024
+BATCH_TILES = BATCH // P
+FEATURE_TILES = FEATURES // P
+SOURCES = 2
+SOURCE_PASSES = FEATURES // (P * PACK)
+PASSES = SOURCES * SOURCE_PASSES
+WORDS = FEATURES // 2
+WORD_BLOCKS = WORDS // P
+GATES = 2
+N_FLOOR = 1e-6
+STORE_TILES = 2
+
+FLOPS = 2 * BATCH * (SOURCES * FEATURES) * (GATES * FEATURES)
+
+
+def tile_slstmlayer_pb_kernel(
+    tc, x, h_prev, c_prev, n_prev, i_prime, f_prime, Wz_x, b_z, Wz_h, Wo_x, b_o, Wo_h, out_0, out_1
+):
+    nc = tc.nc
+    gate_function = (ACT.Tanh, ACT.Sigmoid)
+
+    def by_batch_tile(dram):
+        return dram.rearrange("(p t) f -> p t f", t=BATCH_TILES)
+
+    with ExitStack() as ctx:
+        ctx.enter_context(tc.manual_schedule())
+        keep = ctx.enter_context(tc.tile_pool(name="keep", bufs=1))
+        regrouped = ctx.enter_context(tc.tile_pool(name="regrouped", bufs=2))
+        quantised = ctx.enter_context(tc.tile_pool(name="quantised", bufs=4))
+        work = ctx.enter_context(tc.tile_pool(name="work", bufs=2))
+        flipped_banks = ctx.enter_context(tc.psum_pool(name="flipped_banks", bufs=4))
+        product_banks = ctx.enter_context(tc.psum_pool(name="product_banks", bufs=2))
+        gate_banks = ctx.enter_context(tc.psum_pool(name="gate_banks", bufs=2))
+
+        identity = keep.tile([P, P], F32, name="identity")
+        act_raw = [keep.tile([P, BATCH_TILES * FEATURES], BF16, name="act_raw%d" % s) for s in range(SOURCES)]
+        w_raw = [
+            [keep.tile([P, FEATURE_TILES * FEATURES], BF16, name="w_raw%d%d" % (gate, s)) for s in range(SOURCES)]
+            for gate in range(GATES)
+        ]
+        f_sb = keep.tile([P, BATCH_TILES, FEATURES], BF16, name="f_sb")
+        n_sb = keep.tile([P, BATCH_TILES, FEATURES], BF16, name="n_sb")
+        i_sb = keep.tile([P, BATCH_TILES, FEATURES], BF16, name="i_sb")
+        c_sb = keep.tile([P, BATCH_TILES, FEATURES], BF16, name="c_sb")
+        cell = keep.tile([P, BATCH_TILES, FEATURES], F32, name="cell")
+        readout = keep.tile([P, BATCH_TILES, FEATURES], F32, name="readout")
+        act_grouped = [
+            keep.tile([P, SOURCE_PASSES * BATCH * PACK], BF16, name="act_grouped%d" % s, align_bytes=64)
+            for s in range(SOURCES)
+        ]
+        act_codes = keep.tile([P, PASSES, BATCH], U32, name="act_codes", align_bytes=64)
+        act_scales = keep.tile([P, PASSES, BATCH], U8, name="act_scales", align_bytes=64)
+
+        ones = keep.tile([P, 1], F32, name="ones")
+        warm = keep.tile([P, 1], F32, name="warm")
+        nc.vector.memset(ones[:], 1.0)
+        nc.scalar.activation(out=warm[:], in_=ones[:], func=ACT.Abs_reciprocal_sqrt)
+        make_identity(nc, identity[:])
+        bias_rows = keep.tile([P, P], BF16, name="bias_rows")
+        nc.vector.memset(bias_rows[:], 0.0)
+        for gate, bias in enumerate((b_z, b_o)):
+            nc.scalar.dma_start(
+                out=bias_rows[gate * FEATURE_TILES : (gate + 1) * FEATURE_TILES, :],
+                in_=bias.rearrange("(r c) -> r c", c=P),
+            )
+
+        for half in range(2):
+            tiles = slice(half * BATCH_TILES // 2, (half + 1) * BATCH_TILES // 2)
+            for sbuf, dram in ((f_sb, f_prime), (n_sb, n_prev), (i_sb, i_prime)):
+                nc.sync.dma_start(out=sbuf[:, tiles, :], in_=by_batch_tile(dram)[:, tiles, :])
+        for s, dram in enumerate((x, h_prev)):
+            nc.sync.dma_start(
+                out=act_raw[s][:].rearrange("p (t f) -> p t f", t=BATCH_TILES), in_=by_batch_tile(dram)
+            )
+
+        def load_weights(ft):
+            for gate, pair in enumerate(((Wz_x, Wz_h), (Wo_x, Wo_h))):
+                for s, dram in enumerate(pair):
+                    nc.sync.dma_start(
+                        out=w_raw[gate][s][:, ft * FEATURES : (ft + 1) * FEATURES],
+                        in_=dram[ft * P : (ft + 1) * P, :],
+                    )
+
+        load_weights(0)
+        nc.sync.dma_start(out=c_sb[:], in_=by_batch_tile(c_prev))
+        for ft in range(1, FEATURE_TILES):
+            load_weights(ft)
+
+        def regroup_rows(words, grouped_words):
+            bank = flipped_banks.tile([P, WORD_BLOCKS, P], F32, name="flipped")
+            for j in range(WORD_BLOCKS):
+                nc.tensor.transpose(bank[:, j, :], words[:, j * P : (j + 1) * P], identity[:])
+            nc.scalar.copy(out=grouped_words, in_=bank[:].rearrange("q (g u) r -> q g r u", u=2))
+
+        def normaliser(tiles):
+            for t in tiles:
+                nc.vector.tensor_tensor(out=readout[:, t, :], in0=f_sb[:, t, :], in1=n_sb[:, t, :], op=ALU.mult)
+            for t in tiles:
+                nc.vector.tensor_tensor(out=readout[:, t, :], in0=readout[:, t, :], in1=i_sb[:, t, :], op=ALU.add)
+            for t in tiles:
+                nc.vector.tensor_scalar_max(out=readout[:, t, :], in0=readout[:, t, :], scalar1=N_FLOOR)
+
+        def reciprocal_root(tiles):
+            for t in tiles:
+                nc.scalar.activation(out=readout[:, t, :], in_=readout[:, t, :], func=ACT.Abs_reciprocal_sqrt)
+
+        def quantise_activations(s):
+            for g in range(SOURCE_PASSES):
+                nc.vector.quantize_mx(
+                    out=act_codes[:, s * SOURCE_PASSES + g, :].bitcast(FP8X4),
+                    scales=act_scales[:, s * SOURCE_PASSES + g, :],
+                    in_=act_grouped[s][:, g * BATCH * PACK : (g + 1) * BATCH * PACK],
+                )
+
+        w_grouped = {}
+        w_codes = {}
+        w_scales = {}
+        gate_rows = {}
+        gate_cols = {}
+
+        def transpose_weights(ft, gate):
+            grouped = regrouped.tile([P, PASSES * P * PACK], BF16, name="w_grouped", align_bytes=64)
+            grouped_words = grouped[:].bitcast(F32).rearrange("q (s g r u) -> q s g r u", s=SOURCES, g=SOURCE_PASSES, u=2)
+            for s in range(SOURCES):
+                words = w_raw[gate][s][:].bitcast(F32)[:, ft * WORDS : (ft + 1) * WORDS]
+                regroup_rows(words, grouped_words[:, s])
+            w_grouped[(ft, gate)] = grouped
+
+        def quantise_weights(ft, gate):
+            codes = quantised.tile([P, PASSES * P], U32, name="w_codes", align_bytes=64)
+            scales = quantised.tile([P, PASSES * P], U8, name="w_scales", align_bytes=64)
+            nc.vector.quantize_mx(out=codes[:].bitcast(FP8X4), scales=scales[:], in_=w_grouped[(ft, gate)][:])
+            w_codes[(ft, gate)] = codes
+            w_scales[(ft, gate)] = scales
+
+        def multiply_and_activate(ft, gate):
+            product = product_banks.tile([P, BATCH], F32, name="product")
+            for k in range(PASSES):
+                columns = slice(k * P, (k + 1) * P)
+                nc.tensor.matmul_mx(
+                    out=product[:],
+                    lhsT=w_codes[(ft, gate)][:, columns].bitcast(FP8X4),
+                    lhsT_scale=w_scales[(ft, gate)][:, columns],
+                    rhs=act_codes[:, k, :].bitcast(FP8X4),
+                    rhs_scale=act_scales[:, k, :],
+                    start=(k == 0),
+                    stop=(k == PASSES - 1),
+                )
+            rows = work.tile([P, BATCH], F32, name="gate_rows")
+            column = gate * FEATURE_TILES + ft
+            nc.scalar.activation(
+                out=rows[:], in_=product[:], func=gate_function[gate], bias=bias_cols[:, column : column + 1]
+            )
+            gate_rows[(ft, gate)] = rows
+
+        def transpose_back(ft, gate):
+            bank = gate_banks.tile([P, BATCH_TILES, P], F32, name="gate_cols")
+            for t in range(BATCH_TILES):
+                nc.tensor.transpose(bank[:, t, :], gate_rows[(ft, gate)][:, t * P : (t + 1) * P], identity[:])
+            gate_cols[(ft, gate)] = bank
+
+        def prepare_states(ft):
+            cols = slice(ft * P, (ft + 1) * P)
+            nc.scalar.activation(out=readout[:, :, cols], in_=readout[:, :, cols], func=ACT.Square)
+            nc.vector.tensor_tensor(out=cell[:, :, cols], in0=f_sb[:, :, cols], in1=c_sb[:, :, cols], op=ALU.mult)
+
+        def cell_update(ft):
+            cols = slice(ft * P, (ft + 1) * P)
+            input_term = work.tile([P, BATCH_TILES, P], F32, name="input_term")
+            nc.vector.tensor_tensor(out=input_term[:], in0=gate_cols[(ft, 0)][:], in1=i_sb[:, :, cols], op=ALU.mult)
+            nc.vector.tensor_tensor(out=readout[:, :, cols], in0=gate_cols[(ft, 1)][:], in1=readout[:, :, cols], op=ALU.mult)
+            nc.vector.tensor_tensor(out=cell[:, :, cols], in0=input_term[:], in1=cell[:, :, cols], op=ALU.add)
+            nc.vector.tensor_tensor(out=readout[:, :, cols], in0=readout[:, :, cols], in1=cell[:, :, cols], op=ALU.mult)
+
+        def store(first_ft):
+            cols = slice(first_ft * P, (first_ft + STORE_TILES) * P)
+            nc.sync.dma_start(out=by_batch_tile(out_1)[:, :, cols], in_=cell[:, :, cols])
+            nc.sync.dma_start(out=by_batch_tile(out_0)[:, :, cols], in_=readout[:, :, cols])
+
+        first_half = range(0, BATCH_TILES // 2)
+        second_half = range(BATCH_TILES // 2, BATCH_TILES)
+        normaliser(first_half)
+        reciprocal_root(first_half)
+
+        bias_rows_f32 = keep.tile([P, P], F32, name="bias_rows_f32")
+        nc.vector.tensor_copy(out=bias_rows_f32[:], in_=bias_rows[:])
+        bias_bank = flipped_banks.tile([P, WORD_BLOCKS, P], F32, name="flipped")
+        nc.tensor.transpose(bias_bank[:, 0, :], bias_rows_f32[:], identity[:])
+        bias_cols = keep.tile([P, GATES * FEATURE_TILES], F32, name="bias_cols")
+        nc.vector.tensor_copy(out=bias_cols[:], in_=bias_bank[:, 0, 0 : GATES * FEATURE_TILES])
+
+        for s in range(SOURCES):
+            words = act_raw[s][:].bitcast(F32).rearrange("p (t w) -> p t w", t=BATCH_TILES)
+            grouped_words = act_grouped[s][:].bitcast(F32).rearrange(
+                "q (g t r u) -> q g t r u", g=SOURCE_PASSES, t=BATCH_TILES, u=2
+            )
+            for t in range(BATCH_TILES):
+                regroup_rows(words[:, t, :], grouped_words[:, :, t])
+        normaliser(second_half)
+        reciprocal_root(second_half)
+        for s in range(SOURCES):
+            quantise_activations(s)
+
+        for ft in range(-1, FEATURE_TILES + 1):
+            ahead = ft + 1
+            behind = ft - 1
+            if ahead < FEATURE_TILES:
+                for gate in range(GATES):
+                    transpose_weights(ahead, gate)
+            if behind >= 0:
+                for gate in range(GATES):
+                    transpose_back(behind, gate)
+            if ahead < FEATURE_TILES:
+                for gate in range(GATES):
+                    quantise_weights(ahead, gate)
+                prepare_states(ahead)
+            if behind >= 0:
+                cell_update(behind)
+                if (behind + 1) % STORE_TILES == 0:
+                    store(behind + 1 - STORE_TILES)
+            if 0 <= ft < FEATURE_TILES:
+                for gate in range(GATES):
+                    multiply_and_activate(ft, gate)

@@ -24,7 +24,6 @@ WORDS = FEATURES // 2
 WORD_BLOCKS = WORDS // P
 GATES = 2
 N_FLOOR = 1e-6
-STORE_TILES = 2
 
 FLOPS = 2 * BATCH * (SOURCES * FEATURES) * (GATES * FEATURES)
 
@@ -80,13 +79,12 @@ def tile_slstmlayer_pb_kernel(
                 in_=bias.rearrange("(r c) -> r c", c=P),
             )
 
-        for half in range(2):
+        for half, dram_act in enumerate((x, h_prev)):
             tiles = slice(half * BATCH_TILES // 2, (half + 1) * BATCH_TILES // 2)
             for sbuf, dram in ((f_sb, f_prime), (n_sb, n_prev), (i_sb, i_prime)):
                 nc.sync.dma_start(out=sbuf[:, tiles, :], in_=by_batch_tile(dram)[:, tiles, :])
-        for s, dram in enumerate((x, h_prev)):
             nc.sync.dma_start(
-                out=act_raw[s][:].rearrange("p (t f) -> p t f", t=BATCH_TILES), in_=by_batch_tile(dram)
+                out=act_raw[half][:].rearrange("p (t f) -> p t f", t=BATCH_TILES), in_=by_batch_tile(dram_act)
             )
 
         def load_weights(ft):
@@ -102,11 +100,14 @@ def tile_slstmlayer_pb_kernel(
         for ft in range(1, FEATURE_TILES):
             load_weights(ft)
 
-        def regroup_rows(words, grouped_words):
+        def regroup_rows(words, grouped_words, on_vector=False):
             bank = flipped_banks.tile([P, WORD_BLOCKS, P], F32, name="flipped")
             for j in range(WORD_BLOCKS):
                 nc.tensor.transpose(bank[:, j, :], words[:, j * P : (j + 1) * P], identity[:])
-            nc.scalar.copy(out=grouped_words, in_=bank[:].rearrange("q (g u) r -> q g r u", u=2))
+            if on_vector:
+                nc.vector.tensor_copy(out=grouped_words, in_=bank[:].rearrange("q (g u) r -> q g r u", u=2))
+            else:
+                nc.scalar.copy(out=grouped_words, in_=bank[:].rearrange("q (g u) r -> q g r u", u=2))
 
         def normaliser(tiles):
             for t in tiles:
@@ -139,7 +140,7 @@ def tile_slstmlayer_pb_kernel(
             grouped_words = grouped[:].bitcast(F32).rearrange("q (s g r u) -> q s g r u", s=SOURCES, g=SOURCE_PASSES, u=2)
             for s in range(SOURCES):
                 words = w_raw[gate][s][:].bitcast(F32)[:, ft * WORDS : (ft + 1) * WORDS]
-                regroup_rows(words, grouped_words[:, s])
+                regroup_rows(words, grouped_words[:, s], on_vector=(gate == GATES - 1 and s == SOURCES - 1))
             w_grouped[(ft, gate)] = grouped
 
         def quantise_weights(ft, gate):
@@ -178,25 +179,26 @@ def tile_slstmlayer_pb_kernel(
         def prepare_states(ft):
             cols = slice(ft * P, (ft + 1) * P)
             nc.scalar.activation(out=readout[:, :, cols], in_=readout[:, :, cols], func=ACT.Square)
-            nc.vector.tensor_tensor(out=cell[:, :, cols], in0=f_sb[:, :, cols], in1=c_sb[:, :, cols], op=ALU.mult)
+            nc.gpsimd.tensor_tensor(out=cell[:, :, cols], in0=f_sb[:, :, cols], in1=c_sb[:, :, cols], op=ALU.mult)
 
-        def cell_update(ft):
+        input_terms = {}
+
+        def gate_products(ft):
             cols = slice(ft * P, (ft + 1) * P)
             input_term = work.tile([P, BATCH_TILES, P], F32, name="input_term")
             nc.vector.tensor_tensor(out=input_term[:], in0=gate_cols[(ft, 0)][:], in1=i_sb[:, :, cols], op=ALU.mult)
             nc.vector.tensor_tensor(out=readout[:, :, cols], in0=gate_cols[(ft, 1)][:], in1=readout[:, :, cols], op=ALU.mult)
-            nc.vector.tensor_tensor(out=cell[:, :, cols], in0=input_term[:], in1=cell[:, :, cols], op=ALU.add)
-            nc.vector.tensor_tensor(out=readout[:, :, cols], in0=readout[:, :, cols], in1=cell[:, :, cols], op=ALU.mult)
+            input_terms[ft] = input_term
 
-        def store(first_ft):
-            cols = slice(first_ft * P, (first_ft + STORE_TILES) * P)
+        def finish_cell(ft):
+            cols = slice(ft * P, (ft + 1) * P)
+            nc.vector.tensor_tensor(out=cell[:, :, cols], in0=input_terms[ft][:], in1=cell[:, :, cols], op=ALU.add)
             nc.sync.dma_start(out=by_batch_tile(out_1)[:, :, cols], in_=cell[:, :, cols])
-            nc.sync.dma_start(out=by_batch_tile(out_0)[:, :, cols], in_=readout[:, :, cols])
 
-        first_half = range(0, BATCH_TILES // 2)
-        second_half = range(BATCH_TILES // 2, BATCH_TILES)
-        normaliser(first_half)
-        reciprocal_root(first_half)
+        def finish_readout(ft):
+            cols = slice(ft * P, (ft + 1) * P)
+            nc.vector.tensor_tensor(out=readout[:, :, cols], in0=readout[:, :, cols], in1=cell[:, :, cols], op=ALU.mult)
+            nc.sync.dma_start(out=by_batch_tile(out_0)[:, :, cols], in_=readout[:, :, cols])
 
         bias_rows_f32 = keep.tile([P, P], F32, name="bias_rows_f32")
         nc.vector.tensor_copy(out=bias_rows_f32[:], in_=bias_rows[:])
@@ -206,14 +208,15 @@ def tile_slstmlayer_pb_kernel(
         nc.vector.tensor_copy(out=bias_cols[:], in_=bias_bank[:, 0, 0 : GATES * FEATURE_TILES])
 
         for s in range(SOURCES):
+            half = range(s * BATCH_TILES // 2, (s + 1) * BATCH_TILES // 2)
+            normaliser(half)
             words = act_raw[s][:].bitcast(F32).rearrange("p (t w) -> p t w", t=BATCH_TILES)
             grouped_words = act_grouped[s][:].bitcast(F32).rearrange(
                 "q (g t r u) -> q g t r u", g=SOURCE_PASSES, t=BATCH_TILES, u=2
             )
             for t in range(BATCH_TILES):
                 regroup_rows(words[:, t, :], grouped_words[:, :, t])
-        normaliser(second_half)
-        reciprocal_root(second_half)
+            reciprocal_root(half)
         for s in range(SOURCES):
             quantise_activations(s)
 
@@ -227,13 +230,15 @@ def tile_slstmlayer_pb_kernel(
                 for gate in range(GATES):
                     transpose_back(behind, gate)
             if ahead < FEATURE_TILES:
-                for gate in range(GATES):
-                    quantise_weights(ahead, gate)
+                quantise_weights(ahead, 0)
                 prepare_states(ahead)
             if behind >= 0:
-                cell_update(behind)
-                if (behind + 1) % STORE_TILES == 0:
-                    store(behind + 1 - STORE_TILES)
+                gate_products(behind)
+                finish_cell(behind)
+            if ahead < FEATURE_TILES:
+                quantise_weights(ahead, 1)
+            if behind >= 0:
+                finish_readout(behind)
             if 0 <= ft < FEATURE_TILES:
                 for gate in range(GATES):
                     multiply_and_activate(ft, gate)

@@ -40,7 +40,7 @@ def tile_slstmlayer_pb_kernel(
     with ExitStack() as ctx:
         ctx.enter_context(tc.manual_schedule())
         keep = ctx.enter_context(tc.tile_pool(name="keep", bufs=1))
-        regrouped = ctx.enter_context(tc.tile_pool(name="regrouped", bufs=2))
+        regrouped = ctx.enter_context(tc.tile_pool(name="regrouped", bufs=4))
         quantised = ctx.enter_context(tc.tile_pool(name="quantised", bufs=4))
         work = ctx.enter_context(tc.tile_pool(name="work", bufs=2))
         flipped_banks = ctx.enter_context(tc.psum_pool(name="flipped_banks", bufs=4))
@@ -79,14 +79,6 @@ def tile_slstmlayer_pb_kernel(
                 in_=bias.rearrange("(r c) -> r c", c=P),
             )
 
-        for half, dram_act in enumerate((x, h_prev)):
-            tiles = slice(half * BATCH_TILES // 2, (half + 1) * BATCH_TILES // 2)
-            for sbuf, dram in ((f_sb, f_prime), (n_sb, n_prev), (i_sb, i_prime)):
-                nc.sync.dma_start(out=sbuf[:, tiles, :], in_=by_batch_tile(dram)[:, tiles, :])
-            nc.sync.dma_start(
-                out=act_raw[half][:].rearrange("p (t f) -> p t f", t=BATCH_TILES), in_=by_batch_tile(dram_act)
-            )
-
         def load_weights(ft):
             for gate, pair in enumerate(((Wz_x, Wz_h), (Wo_x, Wo_h))):
                 for s, dram in enumerate(pair):
@@ -95,9 +87,25 @@ def tile_slstmlayer_pb_kernel(
                         in_=dram[ft * P : (ft + 1) * P, :],
                     )
 
+        def load_gates(tiles):
+            for t in tiles:
+                for sbuf, dram in ((f_sb, f_prime), (n_sb, n_prev)):
+                    nc.sync.dma_start(out=sbuf[:, t, :], in_=by_batch_tile(dram)[:, t, :])
+            for t in tiles:
+                nc.sync.dma_start(out=i_sb[:, t, :], in_=by_batch_tile(i_prime)[:, t, :])
+
+        def load_activations(s, dram):
+            nc.sync.dma_start(out=act_raw[s][:].rearrange("p (t f) -> p t f", t=BATCH_TILES), in_=by_batch_tile(dram))
+
+        load_gates(range(0, BATCH_TILES // 2))
+        load_activations(0, x)
+        load_gates(range(BATCH_TILES // 2, BATCH_TILES))
         load_weights(0)
+        load_activations(1, h_prev)
+        load_weights(1)
+        load_weights(2)
         nc.sync.dma_start(out=c_sb[:], in_=by_batch_tile(c_prev))
-        for ft in range(1, FEATURE_TILES):
+        for ft in range(3, FEATURE_TILES):
             load_weights(ft)
 
         def regroup_rows(words, grouped_words, on_vector=False):
@@ -140,7 +148,7 @@ def tile_slstmlayer_pb_kernel(
             grouped_words = grouped[:].bitcast(F32).rearrange("q (s g r u) -> q s g r u", s=SOURCES, g=SOURCE_PASSES, u=2)
             for s in range(SOURCES):
                 words = w_raw[gate][s][:].bitcast(F32)[:, ft * WORDS : (ft + 1) * WORDS]
-                regroup_rows(words, grouped_words[:, s], on_vector=(gate == GATES - 1 and s == SOURCES - 1))
+                regroup_rows(words, grouped_words[:, s])
             w_grouped[(ft, gate)] = grouped
 
         def quantise_weights(ft, gate):
@@ -176,10 +184,14 @@ def tile_slstmlayer_pb_kernel(
                 nc.tensor.transpose(bank[:, t, :], gate_rows[(ft, gate)][:, t * P : (t + 1) * P], identity[:])
             gate_cols[(ft, gate)] = bank
 
+        kept_terms = {}
+
         def prepare_states(ft):
             cols = slice(ft * P, (ft + 1) * P)
             nc.scalar.activation(out=readout[:, :, cols], in_=readout[:, :, cols], func=ACT.Square)
-            nc.gpsimd.tensor_tensor(out=cell[:, :, cols], in0=f_sb[:, :, cols], in1=c_sb[:, :, cols], op=ALU.mult)
+            kept = work.tile([P, BATCH_TILES, P], F32, name="kept_term")
+            nc.gpsimd.tensor_tensor(out=kept[:], in0=f_sb[:, :, cols], in1=c_sb[:, :, cols], op=ALU.mult)
+            kept_terms[ft] = kept
 
         input_terms = {}
 
@@ -192,7 +204,7 @@ def tile_slstmlayer_pb_kernel(
 
         def finish_cell(ft):
             cols = slice(ft * P, (ft + 1) * P)
-            nc.vector.tensor_tensor(out=cell[:, :, cols], in0=input_terms[ft][:], in1=cell[:, :, cols], op=ALU.add)
+            nc.vector.tensor_tensor(out=cell[:, :, cols], in0=input_terms[ft][:], in1=kept_terms[ft][:], op=ALU.add)
             nc.sync.dma_start(out=by_batch_tile(out_1)[:, :, cols], in_=cell[:, :, cols])
 
         def finish_readout(ft):
@@ -200,27 +212,35 @@ def tile_slstmlayer_pb_kernel(
             nc.vector.tensor_tensor(out=readout[:, :, cols], in0=readout[:, :, cols], in1=cell[:, :, cols], op=ALU.mult)
             nc.sync.dma_start(out=by_batch_tile(out_0)[:, :, cols], in_=readout[:, :, cols])
 
+        def regroup_activations(s):
+            words = act_raw[s][:].bitcast(F32).rearrange("p (t w) -> p t w", t=BATCH_TILES)
+            grouped_words = act_grouped[s][:].bitcast(F32).rearrange(
+                "q (g t r u) -> q g t r u", g=SOURCE_PASSES, t=BATCH_TILES, u=2
+            )
+            for t in range(BATCH_TILES):
+                regroup_rows(words[:, t, :], grouped_words[:, :, t], on_vector=(s == SOURCES - 1 and t % 2 == 1))
+
+        normaliser(range(0, BATCH_TILES // 2))
+        regroup_activations(0)
+        reciprocal_root(range(0, BATCH_TILES // 2))
         bias_rows_f32 = keep.tile([P, P], F32, name="bias_rows_f32")
         nc.vector.tensor_copy(out=bias_rows_f32[:], in_=bias_rows[:])
         bias_bank = flipped_banks.tile([P, WORD_BLOCKS, P], F32, name="flipped")
         nc.tensor.transpose(bias_bank[:, 0, :], bias_rows_f32[:], identity[:])
         bias_cols = keep.tile([P, GATES * FEATURE_TILES], F32, name="bias_cols")
         nc.vector.tensor_copy(out=bias_cols[:], in_=bias_bank[:, 0, 0 : GATES * FEATURE_TILES])
+        normaliser(range(BATCH_TILES // 2, BATCH_TILES))
+        quantise_activations(0)
+        for gate in range(GATES):
+            transpose_weights(0, gate)
+        reciprocal_root(range(BATCH_TILES // 2, BATCH_TILES))
+        for gate in range(GATES):
+            quantise_weights(0, gate)
+        regroup_activations(1)
+        quantise_activations(1)
+        prepare_states(0)
 
-        for s in range(SOURCES):
-            half = range(s * BATCH_TILES // 2, (s + 1) * BATCH_TILES // 2)
-            normaliser(half)
-            words = act_raw[s][:].bitcast(F32).rearrange("p (t w) -> p t w", t=BATCH_TILES)
-            grouped_words = act_grouped[s][:].bitcast(F32).rearrange(
-                "q (g t r u) -> q g t r u", g=SOURCE_PASSES, t=BATCH_TILES, u=2
-            )
-            for t in range(BATCH_TILES):
-                regroup_rows(words[:, t, :], grouped_words[:, :, t])
-            reciprocal_root(half)
-        for s in range(SOURCES):
-            quantise_activations(s)
-
-        for ft in range(-1, FEATURE_TILES + 1):
+        for ft in range(0, FEATURE_TILES + 1):
             ahead = ft + 1
             behind = ft - 1
             if ahead < FEATURE_TILES:
@@ -231,7 +251,6 @@ def tile_slstmlayer_pb_kernel(
                     transpose_back(behind, gate)
             if ahead < FEATURE_TILES:
                 quantise_weights(ahead, 0)
-                prepare_states(ahead)
             if behind >= 0:
                 gate_products(behind)
                 finish_cell(behind)
@@ -242,3 +261,5 @@ def tile_slstmlayer_pb_kernel(
             if 0 <= ft < FEATURE_TILES:
                 for gate in range(GATES):
                     multiply_and_activate(ft, gate)
+            if ahead < FEATURE_TILES:
+                prepare_states(ahead)

from contextlib import ExitStack

import concourse.mybir as mybir
from concourse.masks import make_identity

F32 = mybir.dt.float32
BF16 = mybir.dt.bfloat16
U32 = mybir.dt.uint32
U8 = mybir.dt.uint8
FP8X4 = mybir.dt.float8_e4m3fn_x4
ACT = mybir.ActivationFunctionType
ALU = mybir.AluOpType

P = 128
PACK = 4
BATCH = 512
FEATURES = 1024
BATCH_TILES = BATCH // P
FEATURE_TILES = FEATURES // P
SOURCES = 2
SOURCE_PASSES = FEATURES // (P * PACK)
PASSES = SOURCES * SOURCE_PASSES
WORDS = FEATURES // 2
WORD_BLOCKS = WORDS // P
GATES = 2
N_FLOOR = 1e-6

FLOPS = 2 * BATCH * (SOURCES * FEATURES) * (GATES * FEATURES)


def tile_slstmlayer_pb_kernel(
    tc, x, h_prev, c_prev, n_prev, i_prime, f_prime, Wz_x, b_z, Wz_h, Wo_x, b_o, Wo_h, out_0, out_1
):
    nc = tc.nc
    gate_function = (ACT.Tanh, ACT.Sigmoid)

    def by_batch_tile(dram):
        return dram.rearrange("(p t) f -> p t f", t=BATCH_TILES)

    with ExitStack() as ctx:
        ctx.enter_context(tc.manual_schedule())
        keep = ctx.enter_context(tc.tile_pool(name="keep", bufs=1))
        regrouped = ctx.enter_context(tc.tile_pool(name="regrouped", bufs=4))
        quantised = ctx.enter_context(tc.tile_pool(name="quantised", bufs=4))
        work = ctx.enter_context(tc.tile_pool(name="work", bufs=2))
        flipped_banks = ctx.enter_context(tc.psum_pool(name="flipped_banks", bufs=4))
        product_banks = ctx.enter_context(tc.psum_pool(name="product_banks", bufs=2))
        gate_banks = ctx.enter_context(tc.psum_pool(name="gate_banks", bufs=2))

        identity = keep.tile([P, P], F32, name="identity")
        act_raw = [keep.tile([P, BATCH_TILES * FEATURES], BF16, name="act_raw%d" % s) for s in range(SOURCES)]
        w_raw = [
            [keep.tile([P, FEATURE_TILES * FEATURES], BF16, name="w_raw%d%d" % (gate, s)) for s in range(SOURCES)]
            for gate in range(GATES)
        ]
        f_sb = keep.tile([P, BATCH_TILES, FEATURES], BF16, name="f_sb")
        n_sb = keep.tile([P, BATCH_TILES, FEATURES], BF16, name="n_sb")
        i_sb = keep.tile([P, BATCH_TILES, FEATURES], BF16, name="i_sb")
        c_sb = keep.tile([P, BATCH_TILES, FEATURES], BF16, name="c_sb")
        cell = keep.tile([P, BATCH_TILES, FEATURES], F32, name="cell")
        readout = keep.tile([P, BATCH_TILES, FEATURES], F32, name="readout")
        act_grouped = [
            keep.tile([P, SOURCE_PASSES * BATCH * PACK], BF16, name="act_grouped%d" % s, align_bytes=64)
            for s in range(SOURCES)
        ]
        act_codes = keep.tile([P, PASSES, BATCH], U32, name="act_codes", align_bytes=64)
        act_scales = keep.tile([P, PASSES, BATCH], U8, name="act_scales", align_bytes=64)

        ones = keep.tile([P, 1], F32, name="ones")
        warm = keep.tile([P, 1], F32, name="warm")
        nc.vector.memset(ones[:], 1.0)
        nc.scalar.activation(out=warm[:], in_=ones[:], func=ACT.Abs_reciprocal_sqrt)
        make_identity(nc, identity[:])
        bias_rows = keep.tile([P, P], BF16, name="bias_rows")
        nc.vector.memset(bias_rows[:], 0.0)
        for gate, bias in enumerate((b_z, b_o)):
            nc.scalar.dma_start(
                out=bias_rows[gate * FEATURE_TILES : (gate + 1) * FEATURE_TILES, :],
                in_=bias.rearrange("(r c) -> r c", c=P),
            )

        def load_weights(ft):
            for gate, pair in enumerate(((Wz_x, Wz_h), (Wo_x, Wo_h))):
                for s, dram in enumerate(pair):
                    nc.sync.dma_start(
                        out=w_raw[gate][s][:, ft * FEATURES : (ft + 1) * FEATURES],
                        in_=dram[ft * P : (ft + 1) * P, :],
                    )

        def load_gates(tiles):
            for t in tiles:
                for sbuf, dram in ((f_sb, f_prime), (n_sb, n_prev)):
                    nc.sync.dma_start(out=sbuf[:, t, :], in_=by_batch_tile(dram)[:, t, :])
            for t in tiles:
                nc.sync.dma_start(out=i_sb[:, t, :], in_=by_batch_tile(i_prime)[:, t, :])

        def load_activations(s, dram):
            nc.sync.dma_start(out=act_raw[s][:].rearrange("p (t f) -> p t f", t=BATCH_TILES), in_=by_batch_tile(dram))

        load_gates(range(0, BATCH_TILES // 2))
        load_activations(0, x)
        load_gates(range(BATCH_TILES // 2, BATCH_TILES))
        load_weights(0)
        load_activations(1, h_prev)
        load_weights(1)
        load_weights(2)
        nc.sync.dma_start(out=c_sb[:], in_=by_batch_tile(c_prev))
        for ft in range(3, FEATURE_TILES):
            load_weights(ft)

        def regroup_rows(words, grouped_words, on_vector=False):
            bank = flipped_banks.tile([P, WORD_BLOCKS, P], F32, name="flipped")
            for j in range(WORD_BLOCKS):
                nc.tensor.transpose(bank[:, j, :], words[:, j * P : (j + 1) * P], identity[:])
            if on_vector:
                nc.vector.tensor_copy(out=grouped_words, in_=bank[:].rearrange("q (g u) r -> q g r u", u=2))
            else:
                nc.scalar.copy(out=grouped_words, in_=bank[:].rearrange("q (g u) r -> q g r u", u=2))

        def normaliser(tiles):
            for t in tiles:
                nc.vector.tensor_tensor(out=readout[:, t, :], in0=f_sb[:, t, :], in1=n_sb[:, t, :], op=ALU.mult)
            for t in tiles:
                nc.vector.tensor_tensor(out=readout[:, t, :], in0=readout[:, t, :], in1=i_sb[:, t, :], op=ALU.add)
            for t in tiles:
                nc.vector.tensor_scalar_max(out=readout[:, t, :], in0=readout[:, t, :], scalar1=N_FLOOR)

        def reciprocal_root(tiles):
            for t in tiles:
                nc.scalar.activation(out=readout[:, t, :], in_=readout[:, t, :], func=ACT.Abs_reciprocal_sqrt)

        def quantise_activations(s):
            for g in range(SOURCE_PASSES):
                nc.vector.quantize_mx(
                    out=act_codes[:, s * SOURCE_PASSES + g, :].bitcast(FP8X4),
                    scales=act_scales[:, s * SOURCE_PASSES + g, :],
                    in_=act_grouped[s][:, g * BATCH * PACK : (g + 1) * BATCH * PACK],
                )

        w_grouped = {}
        w_codes = {}
        w_scales = {}
        gate_rows = {}
        gate_cols = {}

        def transpose_weights(ft, gate):
            grouped = regrouped.tile([P, PASSES * P * PACK], BF16, name="w_grouped", align_bytes=64)
            grouped_words = grouped[:].bitcast(F32).rearrange("q (s g r u) -> q s g r u", s=SOURCES, g=SOURCE_PASSES, u=2)
            for s in range(SOURCES):
                words = w_raw[gate][s][:].bitcast(F32)[:, ft * WORDS : (ft + 1) * WORDS]
                regroup_rows(words, grouped_words[:, s])
            w_grouped[(ft, gate)] = grouped

        def quantise_weights(ft, gate):
            codes = quantised.tile([P, PASSES * P], U32, name="w_codes", align_bytes=64)
            scales = quantised.tile([P, PASSES * P], U8, name="w_scales", align_bytes=64)
            nc.vector.quantize_mx(out=codes[:].bitcast(FP8X4), scales=scales[:], in_=w_grouped[(ft, gate)][:])
            w_codes[(ft, gate)] = codes
            w_scales[(ft, gate)] = scales

        def multiply_and_activate(ft, gate):
            product = product_banks.tile([P, BATCH], F32, name="product")
            for k in range(PASSES):
                columns = slice(k * P, (k + 1) * P)
                nc.tensor.matmul_mx(
                    out=product[:],
                    lhsT=w_codes[(ft, gate)][:, columns].bitcast(FP8X4),
                    lhsT_scale=w_scales[(ft, gate)][:, columns],
                    rhs=act_codes[:, k, :].bitcast(FP8X4),
                    rhs_scale=act_scales[:, k, :],
                    start=(k == 0),
                    stop=(k == PASSES - 1),
                )
            rows = work.tile([P, BATCH], F32, name="gate_rows")
            column = gate * FEATURE_TILES + ft
            nc.scalar.activation(
                out=rows[:], in_=product[:], func=gate_function[gate], bias=bias_cols[:, column : column + 1]
            )
            gate_rows[(ft, gate)] = rows

        def transpose_back(ft, gate):
            bank = gate_banks.tile([P, BATCH_TILES, P], F32, name="gate_cols")
            for t in range(BATCH_TILES):
                nc.tensor.transpose(bank[:, t, :], gate_rows[(ft, gate)][:, t * P : (t + 1) * P], identity[:])
            gate_cols[(ft, gate)] = bank

        kept_terms = {}

        def prepare_states(ft):
            cols = slice(ft * P, (ft + 1) * P)
            nc.scalar.activation(out=readout[:, :, cols], in_=readout[:, :, cols], func=ACT.Square)
            kept = work.tile([P, BATCH_TILES, P], F32, name="kept_term")
            nc.gpsimd.tensor_tensor(out=kept[:], in0=f_sb[:, :, cols], in1=c_sb[:, :, cols], op=ALU.mult)
            kept_terms[ft] = kept

        input_terms = {}

        def gate_products(ft):
            cols = slice(ft * P, (ft + 1) * P)
            input_term = work.tile([P, BATCH_TILES, P], F32, name="input_term")
            nc.vector.tensor_tensor(out=input_term[:], in0=gate_cols[(ft, 0)][:], in1=i_sb[:, :, cols], op=ALU.mult)
            nc.vector.tensor_tensor(out=readout[:, :, cols], in0=gate_cols[(ft, 1)][:], in1=readout[:, :, cols], op=ALU.mult)
            input_terms[ft] = input_term

        def finish_cell(ft):
            cols = slice(ft * P, (ft + 1) * P)
            nc.vector.tensor_tensor(out=cell[:, :, cols], in0=input_terms[ft][:], in1=kept_terms[ft][:], op=ALU.add)
            nc.sync.dma_start(out=by_batch_tile(out_1)[:, :, cols], in_=cell[:, :, cols])

        def finish_readout(ft):
            cols = slice(ft * P, (ft + 1) * P)
            nc.vector.tensor_tensor(out=readout[:, :, cols], in0=readout[:, :, cols], in1=cell[:, :, cols], op=ALU.mult)
            nc.sync.dma_start(out=by_batch_tile(out_0)[:, :, cols], in_=readout[:, :, cols])

        def regroup_activations(s):
            words = act_raw[s][:].bitcast(F32).rearrange("p (t w) -> p t w", t=BATCH_TILES)
            grouped_words = act_grouped[s][:].bitcast(F32).rearrange(
                "q (g t r u) -> q g t r u", g=SOURCE_PASSES, t=BATCH_TILES, u=2
            )
            for t in range(BATCH_TILES):
                regroup_rows(words[:, t, :], grouped_words[:, :, t], on_vector=(s == SOURCES - 1 and t % 2 == 1))

        normaliser(range(0, BATCH_TILES // 2))
        regroup_activations(0)
        reciprocal_root(range(0, BATCH_TILES // 2))
        bias_rows_f32 = keep.tile([P, P], F32, name="bias_rows_f32")
        nc.vector.tensor_copy(out=bias_rows_f32[:], in_=bias_rows[:])
        bias_bank = flipped_banks.tile([P, WORD_BLOCKS, P], F32, name="flipped")
        nc.tensor.transpose(bias_bank[:, 0, :], bias_rows_f32[:], identity[:])
        bias_cols = keep.tile([P, GATES * FEATURE_TILES], F32, name="bias_cols")
        nc.vector.tensor_copy(out=bias_cols[:], in_=bias_bank[:, 0, 0 : GATES * FEATURE_TILES])
        normaliser(range(BATCH_TILES // 2, BATCH_TILES))
        quantise_activations(0)
        for gate in range(GATES):
            transpose_weights(0, gate)
        reciprocal_root(range(BATCH_TILES // 2, BATCH_TILES))
        for gate in range(GATES):
            quantise_weights(0, gate)
        regroup_activations(1)
        quantise_activations(1)
        prepare_states(0)

        for ft in range(0, FEATURE_TILES + 1):
            ahead = ft + 1
            behind = ft - 1
            if ahead < FEATURE_TILES:
                for gate in range(GATES):
                    transpose_weights(ahead, gate)
            if behind >= 0:
                for gate in range(GATES):
                    transpose_back(behind, gate)
            if ahead < FEATURE_TILES:
                quantise_weights(ahead, 0)
            if behind >= 0:
                gate_products(behind)
                finish_cell(behind)
            if ahead < FEATURE_TILES:
                quantise_weights(ahead, 1)
            if behind >= 0:
                finish_readout(behind)
            if 0 <= ft < FEATURE_TILES:
                for gate in range(GATES):
                    multiply_and_activate(ft, gate)
            if ahead < FEATURE_TILES:
                prepare_states(ahead)
